import numpy as np
import ml_dtypes


def mxq(x, axis, fmt="e4m3"):
    dtype, down = {"e4m3": (ml_dtypes.float8_e4m3fn, 7), "e5m2": (ml_dtypes.float8_e5m2, 14)}[fmt]
    v = np.moveaxis(np.asarray(x, np.float32).astype(ml_dtypes.bfloat16).astype(np.float64), axis, -1)
    blocks = v.reshape(v.shape[:-1] + (-1, 32))
    amax = np.abs(blocks).max(-1, keepdims=True)
    byte = np.maximum(np.where(amax > 0, np.frexp(amax)[1] - 1 + 127, 0) - down, 1)
    scale = np.exp2(byte - 127.0)
    codes = (blocks / scale).astype(np.float32).astype(dtype).astype(np.float64)
    return np.moveaxis((codes * scale).reshape(v.shape), -1, axis)


WIDE = False


def mx_kscale(k):
    if not WIDE:
        return np.ones(k)
    levels = np.array([10, -10, 5, -5, 0])
    if k % 512:
        return np.exp2(np.random.permutation(np.resize(levels, k // 32))).repeat(32)
    a = np.empty((k // 512, 16))
    for p in range(k // 512):
        a[p, :8] = np.random.permutation(np.resize(levels, 8))
        for g in range(8):
            far = levels[np.abs(levels - a[p, g]) >= 10]
            a[p, g + 8] = far[np.random.randint(len(far))]
    return np.exp2(a.ravel()).repeat(32)


BF16 = ml_dtypes.bfloat16


def bf(x):
    return np.asarray(x, np.float32).astype(BF16)


def f64(x):
    return np.asarray(x).astype(np.float64)


T, D, H = 256, 2048, 16
DH = D // H
EPS = 1e-5


def rope_tables():
    inv_freq = 1.0 / (10000.0 ** (np.arange(0, DH, 2) / DH))
    ang = np.outer(np.arange(T), inv_freq)
    ang = np.concatenate([ang, ang], axis=-1)
    return np.cos(ang), np.sin(ang)


def rotate_half(u):
    u1, u2 = np.split(u, 2, axis=-1)
    return np.concatenate((-u2, u1), axis=-1)


def setup_inputs():
    s = mx_kscale(D)
    r = 10.0 ** np.random.uniform(-3.0, 0.0, (T, 1))
    c, sn = rope_tables()
    return {"x": bf(np.random.standard_normal((T, D)) * r),
            "w_ln": bf((1.0 + 0.1 * np.random.standard_normal(D)) * s),
            "wq": bf(np.random.standard_normal((D, D)) / np.sqrt(D) / s[None, :]),
            "wk": bf(np.random.standard_normal((D, D)) / np.sqrt(D) / s[None, :]),
            "wv": bf(np.random.standard_normal((D, D)) / np.sqrt(D) / s[None, :]),
            "cos": bf(c), "sin": bf(sn)}


def reference(x, w_ln, wq, wk, wv, cos, sin):
    x, c, sn = f64(x), f64(cos), f64(sin)
    var = np.mean(x * x, axis=-1, keepdims=True)
    h = f64(w_ln) * x * (1.0 / np.sqrt(var + EPS))
    hq = mxq(h, 1, "e4m3")
    q = (hq @ mxq(f64(wq), 1, "e4m3").T).reshape(T, H, DH).transpose(1, 0, 2)
    k = (hq @ mxq(f64(wk), 1, "e4m3").T).reshape(T, H, DH).transpose(1, 0, 2)
    v = (hq @ mxq(f64(wv), 1, "e4m3").T).reshape(T, H, DH).transpose(1, 0, 2)
    q = q * c + rotate_half(q) * sn
    k = k * c + rotate_half(k) * sn
    return q, k, v

@@ -1,0 +1,253 @@
+from contextlib import ExitStack
+
+import concourse.mybir as mybir
+from concourse.masks import make_identity
+
+F32 = mybir.dt.float32
+BF16 = mybir.dt.bfloat16
+I32 = mybir.dt.int32
+U32 = mybir.dt.uint32
+U8 = mybir.dt.uint8
+FP8X4 = mybir.dt.float8_e4m3fn_x4
+MULT = mybir.AluOpType.mult
+ADD = mybir.AluOpType.add
+ACT = mybir.ActivationFunctionType
+
+P = 128
+T, D, H, DH = 256, 2048, 16, 128
+EPS = 1e-5
+PACK = 4
+K_PASS = P * PACK
+PASSES = D // K_PASS
+TOKEN_TILES = T // P
+HALF = DH // 2
+
+UNIT_HEADS = 2
+UNIT_F = UNIT_HEADS * DH
+UNITS = 3 * H // UNIT_HEADS
+ROUND = 1
+LAG = 2
+H_ROUND = 1
+
+PSUM_BANKS = 8
+ACC_BANKS = 2
+T_BANKS = PSUM_BANKS - ACC_BANKS
+PREFETCH = 8
+RAW_BUFS = PREFETCH + 2
+GROUPED_BUFS = 3
+RES_BUFS = 8
+CODE_BUFS = (LAG + 1) * ROUND + 1
+
+FLOPS = 2 * T * D * 3 * D
+
+
+def unit_order():
+    pairs = H // UNIT_HEADS
+    order = []
+    for pair in range(pairs):
+        order.extend([(0, pair), (1, pair)])
+        if pair > 0:
+            order.append((2, pair - 1))
+    order.append((2, pairs - 1))
+    return order
+
+
+def tile_attention_pa_kernel(tc, x, w_ln, wq, wk, wv, cos, sin, out_0, out_1, out_2):
+    nc = tc.nc
+    weights = (wq, wk, wv)
+    outs = (out_0, out_1, out_2)
+    units = unit_order()
+    with ExitStack() as ctx:
+        ctx.enter_context(tc.manual_schedule())
+        keep = ctx.enter_context(tc.tile_pool(name="keep", bufs=1))
+        raw_pool = ctx.enter_context(tc.tile_pool(name="raw", bufs=RAW_BUFS))
+        grouped_pool = ctx.enter_context(tc.tile_pool(name="grouped", bufs=GROUPED_BUFS))
+        code_pool = ctx.enter_context(tc.tile_pool(name="codes", bufs=CODE_BUFS))
+        res_pool = ctx.enter_context(tc.tile_pool(name="res", bufs=RES_BUFS))
+        far_pool = ctx.enter_context(tc.tile_pool(name="far", bufs=2))
+        t_psum = ctx.enter_context(tc.psum_pool(name="t_psum", bufs=T_BANKS))
+        acc_psum = ctx.enter_context(tc.psum_pool(name="acc_psum", bufs=ACC_BANKS))
+
+        x_rows = x.rearrange("(p two) k -> p two k", two=TOKEN_TILES)
+        x_sb = []
+        for tt in range(TOKEN_TILES):
+            x_tile = keep.tile([P, D], BF16, name="x_sb%d" % tt)
+            nc.sync.dma_start(out=x_tile[:], in_=x_rows[:, tt, :])
+            x_sb.append(x_tile)
+
+        w_row = keep.tile([P, D], BF16, name="w_row")
+        nc.vector.memset(w_row[:].bitcast(I32), 0)
+        nc.sync.dma_start(out=w_row[0:1, :], in_=w_ln.rearrange("(o k) -> o k", o=1))
+        ones = keep.tile([P, P], BF16, name="ones")
+        nc.vector.memset(ones[:], 1.0)
+        cos_sb = keep.tile([P, TOKEN_TILES * DH], BF16, name="cos_sb")
+        nc.scalar.dma_start(out=cos_sb[:], in_=cos.rearrange("(p two) f -> p (two f)", two=TOKEN_TILES))
+        sin_sb = keep.tile([P, TOKEN_TILES * DH], BF16, name="sin_sb")
+        nc.scalar.dma_start(out=sin_sb[:], in_=sin.rearrange("(p two) f -> p (two f)", two=TOKEN_TILES))
+
+        ident_f32 = keep.tile([P, P], F32, name="ident_f32")
+        make_identity(nc, ident_f32[:])
+        ident_bf16 = keep.tile([P, P], BF16, name="ident_bf16")
+        make_identity(nc, ident_bf16[:])
+
+        sin_swap = keep.tile([P, TOKEN_TILES * DH], BF16, name="sin_swap")
+        sin_view = sin_sb[:].rearrange("p (t f) -> p t f", t=TOKEN_TILES)
+        swap_view = sin_swap[:].rearrange("p (t f) -> p t f", t=TOKEN_TILES)
+        nc.gpsimd.tensor_copy(out=swap_view[:, :, 0:HALF], in_=sin_view[:, :, HALF:DH])
+        nc.gpsimd.tensor_scalar(
+            out=swap_view[:, :, HALF:DH], in0=sin_view[:, :, 0:HALF],
+            scalar1=-1.0, scalar2=0.0, op0=MULT, op1=ADD,
+        )
+        table_shape = [P, TOKEN_TILES, UNIT_HEADS, DH]
+        cos_heads = cos_sb[:].rearrange("p (t f) -> p t f", t=TOKEN_TILES).unsqueeze(2).to_broadcast(table_shape)
+        sin_heads = swap_view.unsqueeze(2).to_broadcast(table_shape)
+
+        warm = keep.tile([P, 1], F32, name="warm")
+        nc.scalar.activation(out=warm[:], in_=ones[:, 0:1], func=ACT.Sqrt)
+
+        w_all = keep.tile([P, D], BF16, name="w_all")
+        for c in range(D // 512):
+            cols = slice(512 * c, 512 * (c + 1))
+            w_bank = t_psum.tile([P, 512], F32, name="w_bank", tag="bank")
+            nc.tensor.matmul(out=w_bank[:], lhsT=ones[:], rhs=w_row[:, cols], start=True, stop=True)
+            nc.vector.tensor_copy(out=w_all[:, cols], in_=w_bank[:])
+
+        h_bf = []
+        for tt in range(TOKEN_TILES):
+            squares = keep.tile([P, D], BF16, name="squares%d" % tt)
+            sum_sq = keep.tile([P, 1], F32, name="sum_sq%d" % tt)
+            nc.scalar.activation(out=squares[:], in_=x_sb[tt][:], func=ACT.Square, accum_out=sum_sq[:])
+            mean_sq = keep.tile([P, 1], F32, name="mean_sq%d" % tt)
+            nc.vector.tensor_scalar(out=mean_sq[:], in0=sum_sq[:], scalar1=1.0 / D, scalar2=EPS, op0=MULT, op1=ADD)
+            rms = keep.tile([P, 1], F32, name="rms%d" % tt)
+            nc.scalar.activation(out=rms[:], in_=mean_sq[:], func=ACT.Sqrt)
+            r_col = keep.tile([P, 1], F32, name="r_col%d" % tt)
+            nc.vector.reciprocal(out=r_col[:], in_=rms[:])
+            h_tile = keep.tile([P, D], BF16, name="h_bf%d" % tt)
+            nc.vector.scalar_tensor_tensor(
+                out=h_tile[:], in0=x_sb[tt][:], scalar=r_col[:, 0:1], in1=w_all[:], op0=MULT, op1=MULT,
+            )
+            h_bf.append(h_tile)
+
+        h_grouped = keep.tile([P, PASSES * T * PACK], BF16, name="h_grouped", align_bytes=64)
+        h_codes = keep.tile([P, PASSES * T], U32, name="h_codes", align_bytes=64)
+        h_scales = keep.tile([P, PASSES * T], U8, name="h_scales", align_bytes=64)
+
+        def quantise_h():
+            for tt in range(TOKEN_TILES):
+                for g in range(PASSES):
+                    h_bank = t_psum.tile([P, PACK * P], BF16, name="h_bank", tag="bank")
+                    quads = h_bf[tt][:].rearrange("t (g q j) -> t g j q", q=P, j=PACK)
+                    for j in range(PACK):
+                        nc.tensor.transpose(
+                            h_bank[:, P * j : P * (j + 1)], quads[:, g, j, :], ident_bf16[:]
+                        )
+                    start = (T * g + P * tt) * PACK
+                    nc.vector.tensor_copy(
+                        out=h_grouped[:, start : start + P * PACK].rearrange("q (t j) -> q t j", j=PACK),
+                        in_=h_bank[:].rearrange("q (j t) -> q t j", j=PACK),
+                    )
+            nc.vector.quantize_mx(out=h_codes[:].bitcast(FP8X4), scales=h_scales[:], in_=h_grouped[:])
+
+        raw_of = {}
+        grouped_of = {}
+        codes_of = {}
+        result_of = {}
+
+        def load_unit(n):
+            which, pair = units[n]
+            rows = weights[which][UNIT_F * pair : UNIT_F * (pair + 1), :]
+            w_raw = raw_pool.tile([P, 2 * D], BF16, name="w_raw")
+            nc.sync.dma_start(
+                out=w_raw[:].rearrange("p (n k) -> p n k", n=UNIT_HEADS), in_=rows.rearrange("(n p) k -> p n k", p=P)
+            )
+            raw_of[n] = w_raw
+
+        def transpose_unit(n):
+            words = raw_of.pop(n)[:].bitcast(F32).rearrange("f (n g q u) -> f n g u q", n=UNIT_HEADS, q=P, u=2)
+            grouped = grouped_pool.tile([P, PASSES * UNIT_F * PACK], BF16, name="grouped", align_bytes=64)
+            grouped_words = grouped[:].bitcast(F32)
+            for g in range(PASSES):
+                bank = t_psum.tile([P, 512], F32, name="bank", tag="bank")
+                for u in range(2):
+                    for head in range(UNIT_HEADS):
+                        slot = UNIT_HEADS * u + head
+                        nc.tensor.transpose(
+                            bank[:, P * slot : P * (slot + 1)], words[:, head, g, u, :], ident_f32[:]
+                        )
+                nc.scalar.copy(
+                    out=grouped_words[:, 512 * g : 512 * (g + 1)].rearrange("q (f u) -> q f u", u=2),
+                    in_=bank[:].rearrange("q (u f) -> q f u", u=2),
+                )
+            grouped_of[n] = grouped
+
+        def quantise_unit(n):
+            codes = code_pool.tile([P, PASSES * UNIT_F], U32, name="codes", align_bytes=64)
+            scales = code_pool.tile([P, PASSES * UNIT_F], U8, name="scales", align_bytes=64)
+            nc.vector.quantize_mx(out=codes[:].bitcast(FP8X4), scales=scales[:], in_=grouped_of.pop(n)[:])
+            codes_of[n] = (codes, scales)
+
+        def multiply_unit(n):
+            which = units[n][0]
+            codes, scales = codes_of.pop(n)
+            acc = acc_psum.tile([P, TOKEN_TILES * UNIT_F], F32, name="acc")
+            for tt in range(TOKEN_TILES):
+                for g in range(PASSES):
+                    tokens = slice(T * g + P * tt, T * g + P * (tt + 1))
+                    feats = slice(UNIT_F * g, UNIT_F * (g + 1))
+                    nc.tensor.matmul_mx(
+                        out=acc[:, UNIT_F * tt : UNIT_F * (tt + 1)],
+                        lhsT=h_codes[:, tokens].bitcast(FP8X4),
+                        lhsT_scale=h_scales[:, tokens],
+                        rhs=codes[:, feats].bitcast(FP8X4),
+                        rhs_scale=scales[:, feats],
+                        start=(g == 0),
+                        stop=(g == PASSES - 1),
+                    )
+            acc_view = acc[:].rearrange("p (t h f) -> p t h f", t=TOKEN_TILES, h=UNIT_HEADS)
+            res = res_pool.tile([P, TOKEN_TILES * UNIT_F], F32, name="res")
+            res_view = res[:].rearrange("p (h t f) -> p t h f", h=UNIT_HEADS, t=TOKEN_TILES)
+            if which == 2:
+                nc.scalar.copy(out=res_view, in_=acc_view)
+                result_of[n] = (res, None)
+            else:
+                far = far_pool.tile([P, TOKEN_TILES * UNIT_F], F32, name="far")
+                far_view = far[:].rearrange("p (h t f) -> p t h f", h=UNIT_HEADS, t=TOKEN_TILES)
+                nc.vector.tensor_tensor(out=res_view, in0=acc_view, in1=cos_heads, op=MULT)
+                nc.vector.tensor_tensor(out=far_view, in0=acc_view, in1=sin_heads, op=MULT)
+                result_of[n] = (res, far)
+
+        def finish_unit(n):
+            which, pair = units[n]
+            res, far = result_of.pop(n)
+            if far is not None:
+                res_halves = res[:].rearrange("p (c s j) -> p c s j", s=2, j=HALF)
+                far_halves = far[:].rearrange("p (c s j) -> p c s j", s=2, j=HALF)
+                for s in range(2):
+                    nc.vector.tensor_tensor(
+                        out=res_halves[:, :, s, :], in0=res_halves[:, :, s, :], in1=far_halves[:, :, 1 - s, :], op=ADD,
+                    )
+            heads = outs[which][UNIT_HEADS * pair : UNIT_HEADS * (pair + 1), :, :]
+            nc.sync.dma_start(
+                out=heads.rearrange("h (p t) f -> p h (t f)", t=TOKEN_TILES),
+                in_=res[:].rearrange("p (h c) -> p h c", h=UNIT_HEADS),
+            )
+
+        for n in range(PREFETCH):
+            load_unit(n)
+        rounds = UNITS // ROUND
+        for r in range(rounds + LAG):
+            if r < rounds:
+                for i in range(ROUND):
+                    transpose_unit(ROUND * r + i)
+            if r == H_ROUND:
+                quantise_h()
+            for i in range(ROUND):
+                if r >= LAG:
+                    multiply_unit(ROUND * (r - LAG) + i)
+                if r < rounds:
+                    quantise_unit(ROUND * r + i)
+                if r >= LAG:
+                    finish_unit(ROUND * (r - LAG) + i)
+                if ROUND * r + i + PREFETCH < UNITS:
+                    load_unit(ROUND * r + i + PREFETCH)

@@ -25,18 +25,18 @@ HALF = DH // 2
 UNIT_HEADS = 2
 UNIT_F = UNIT_HEADS * DH
 UNITS = 3 * H // UNIT_HEADS
-ROUND = 1
-LAG = 2
-H_ROUND = 1
+WORDS = UNIT_HEADS * D // 2
 
 PSUM_BANKS = 8
 ACC_BANKS = 2
 T_BANKS = PSUM_BANKS - ACC_BANKS
-PREFETCH = 8
+PREFETCH = 7
 RAW_BUFS = PREFETCH + 2
+SPLIT_BUFS = 4
 GROUPED_BUFS = 3
-RES_BUFS = 8
-CODE_BUFS = (LAG + 1) * ROUND + 1
+RES_BUFS = 6
+CODE_BUFS = 6
+AHEAD = 4
 
 FLOPS = 2 * T * D * 3 * D
 
@@ -52,6 +52,12 @@ def unit_order():
     return order
 
 
+def splitter(n):
+    if n < 2 * AHEAD or n % 3 == 0:
+        return None
+    return "scalar" if n % 4 == 0 else "vector"
+
+
 def tile_attention_pa_kernel(tc, x, w_ln, wq, wk, wv, cos, sin, out_0, out_1, out_2):
     nc = tc.nc
     weights = (wq, wk, wv)
@@ -61,6 +67,7 @@ def tile_attention_pa_kernel(tc, x, w_ln, wq, wk, wv, cos, sin, out_0, out_1, ou
         ctx.enter_context(tc.manual_schedule())
         keep = ctx.enter_context(tc.tile_pool(name="keep", bufs=1))
         raw_pool = ctx.enter_context(tc.tile_pool(name="raw", bufs=RAW_BUFS))
+        split_pool = ctx.enter_context(tc.tile_pool(name="split", bufs=SPLIT_BUFS))
         grouped_pool = ctx.enter_context(tc.tile_pool(name="grouped", bufs=GROUPED_BUFS))
         code_pool = ctx.enter_context(tc.tile_pool(name="codes", bufs=CODE_BUFS))
         res_pool = ctx.enter_context(tc.tile_pool(name="res", bufs=RES_BUFS))
@@ -77,9 +84,9 @@ def tile_attention_pa_kernel(tc, x, w_ln, wq, wk, wv, cos, sin, out_0, out_1, ou
 
         w_row = keep.tile([P, D], BF16, name="w_row")
         nc.vector.memset(w_row[:].bitcast(I32), 0)
-        nc.sync.dma_start(out=w_row[0:1, :], in_=w_ln.rearrange("(o k) -> o k", o=1))
         ones = keep.tile([P, P], BF16, name="ones")
         nc.vector.memset(ones[:], 1.0)
+        nc.sync.dma_start(out=w_row[0:1, :], in_=w_ln.rearrange("(o k) -> o k", o=1))
         cos_sb = keep.tile([P, TOKEN_TILES * DH], BF16, name="cos_sb")
         nc.scalar.dma_start(out=cos_sb[:], in_=cos.rearrange("(p two) f -> p (two f)", two=TOKEN_TILES))
         sin_sb = keep.tile([P, TOKEN_TILES * DH], BF16, name="sin_sb")
@@ -87,8 +94,6 @@ def tile_attention_pa_kernel(tc, x, w_ln, wq, wk, wv, cos, sin, out_0, out_1, ou
 
         ident_f32 = keep.tile([P, P], F32, name="ident_f32")
         make_identity(nc, ident_f32[:])
-        ident_bf16 = keep.tile([P, P], BF16, name="ident_bf16")
-        make_identity(nc, ident_bf16[:])
 
         sin_swap = keep.tile([P, TOKEN_TILES * DH], BF16, name="sin_swap")
         sin_view = sin_sb[:].rearrange("p (t f) -> p t f", t=TOKEN_TILES)
@@ -105,51 +110,86 @@ def tile_attention_pa_kernel(tc, x, w_ln, wq, wk, wv, cos, sin, out_0, out_1, ou
         warm = keep.tile([P, 1], F32, name="warm")
         nc.scalar.activation(out=warm[:], in_=ones[:, 0:1], func=ACT.Sqrt)
 
-        w_all = keep.tile([P, D], BF16, name="w_all")
-        for c in range(D // 512):
-            cols = slice(512 * c, 512 * (c + 1))
-            w_bank = t_psum.tile([P, 512], F32, name="w_bank", tag="bank")
-            nc.tensor.matmul(out=w_bank[:], lhsT=ones[:], rhs=w_row[:, cols], start=True, stop=True)
-            nc.vector.tensor_copy(out=w_all[:, cols], in_=w_bank[:])
+        w_cols = D // ACC_BANKS
+        w_all = []
+        for b in range(ACC_BANKS):
+            w_bank = acc_psum.tile([P, w_cols], BF16, name="w_bank", tag="acc")
+            for c in range(w_cols // 512):
+                first = w_cols * b + 512 * c
+                nc.tensor.matmul(
+                    out=w_bank[:, 512 * c : 512 * (c + 1)], lhsT=ones[:], rhs=w_row[:, first : first + 512],
+                    start=True, stop=True,
+                )
+            w_all.append(w_bank)
 
         h_bf = []
-        for tt in range(TOKEN_TILES):
-            squares = keep.tile([P, D], BF16, name="squares%d" % tt)
-            sum_sq = keep.tile([P, 1], F32, name="sum_sq%d" % tt)
-            nc.scalar.activation(out=squares[:], in_=x_sb[tt][:], func=ACT.Square, accum_out=sum_sq[:])
-            mean_sq = keep.tile([P, 1], F32, name="mean_sq%d" % tt)
-            nc.vector.tensor_scalar(out=mean_sq[:], in0=sum_sq[:], scalar1=1.0 / D, scalar2=EPS, op0=MULT, op1=ADD)
-            rms = keep.tile([P, 1], F32, name="rms%d" % tt)
-            nc.scalar.activation(out=rms[:], in_=mean_sq[:], func=ACT.Sqrt)
-            r_col = keep.tile([P, 1], F32, name="r_col%d" % tt)
-            nc.vector.reciprocal(out=r_col[:], in_=rms[:])
-            h_tile = keep.tile([P, D], BF16, name="h_bf%d" % tt)
-            nc.vector.scalar_tensor_tensor(
-                out=h_tile[:], in0=x_sb[tt][:], scalar=r_col[:, 0:1], in1=w_all[:], op0=MULT, op1=MULT,
-            )
-            h_bf.append(h_tile)
+        h_grouped = keep.tile([P, TOKEN_TILES * PASSES * P * PACK], BF16, name="h_grouped", align_bytes=64)
+        h_codes = keep.tile([P, TOKEN_TILES * PASSES * P], U32, name="h_codes", align_bytes=64)
+        h_scales = keep.tile([P, TOKEN_TILES * PASSES * P], U8, name="h_scales", align_bytes=64)
 
-        h_grouped = keep.tile([P, PASSES * T * PACK], BF16, name="h_grouped", align_bytes=64)
-        h_codes = keep.tile([P, PASSES * T], U32, name="h_codes", align_bytes=64)
-        h_scales = keep.tile([P, PASSES * T], U8, name="h_scales", align_bytes=64)
+        def make_h():
+            squares = keep.tile([P, D], BF16, name="squares")
+            sum_sq = keep.tile([P, 1], F32, name="sum_sq")
+            nc.scalar.activation(out=squares[:], in_=x_sb[0][:], func=ACT.Square, accum_out=sum_sq[:])
+            chunks = D // 512
+            stats = keep.tile([P, chunks * 6], F32, name="stats")
+            for c in range(chunks):
+                nc.vector.bn_stats(out=stats[:, 6 * c : 6 * (c + 1)], in_=x_sb[1][:, 512 * c : 512 * (c + 1)])
+            mean_var = keep.tile([P, 2], F32, name="mean_var")
+            nc.vector.bn_aggr(out=mean_var[:], in_=stats[:])
+            mean_sq = keep.tile([P, TOKEN_TILES], F32, name="mean_sq")
+            nc.vector.tensor_scalar(
+                out=mean_sq[:, 0:1], in0=sum_sq[:], scalar1=1.0 / D, scalar2=EPS, op0=MULT, op1=ADD
+            )
+            power = keep.tile([P, 1], F32, name="power")
+            nc.vector.scalar_tensor_tensor(
+                out=power[:], in0=mean_var[:, 0:1], scalar=mean_var[:, 0:1], in1=mean_var[:, 1:2], op0=MULT, op1=ADD,
+            )
+            nc.vector.tensor_scalar(
+                out=mean_sq[:, 1:2], in0=power[:], scalar1=1.0, scalar2=EPS, op0=MULT, op1=ADD
+            )
+            rms = keep.tile([P, TOKEN_TILES], F32, name="rms")
+            nc.scalar.activation(out=rms[:], in_=mean_sq[:], func=ACT.Sqrt)
+            r_cols = keep.tile([P, TOKEN_TILES], F32, name="r_cols")
+            nc.vector.reciprocal(out=r_cols[:], in_=rms[:])
+            for tt in range(TOKEN_TILES):
+                h_tile = keep.tile([P, D], BF16, name="h_bf%d" % tt)
+                for b in range(ACC_BANKS):
+                    cols = slice(w_cols * b, w_cols * (b + 1))
+                    nc.vector.scalar_tensor_tensor(
+                        out=h_tile[:, cols], in0=x_sb[tt][:, cols], scalar=r_cols[:, tt : tt + 1], in1=w_all[b][:],
+                        op0=MULT, op1=MULT,
+                    )
+                h_bf.append(h_tile)
 
         def quantise_h():
             for tt in range(TOKEN_TILES):
-                for g in range(PASSES):
-                    h_bank = t_psum.tile([P, PACK * P], BF16, name="h_bank", tag="bank")
-                    quads = h_bf[tt][:].rearrange("t (g q j) -> t g j q", q=P, j=PACK)
-                    for j in range(PACK):
-                        nc.tensor.transpose(
-                            h_bank[:, P * j : P * (j + 1)], quads[:, g, j, :], ident_bf16[:]
-                        )
-                    start = (T * g + P * tt) * PACK
-                    nc.vector.tensor_copy(
-                        out=h_grouped[:, start : start + P * PACK].rearrange("q (t j) -> q t j", j=PACK),
-                        in_=h_bank[:].rearrange("q (j t) -> q t j", j=PACK),
+                words = h_bf[tt][:].bitcast(F32).rearrange("t (g q u) -> t g u q", q=P, u=2)
+                grouped_words = h_grouped[:, D * tt : D * (tt + 1)].bitcast(F32)
+                per_bank = 2
+                for first in range(0, PASSES, per_bank):
+                    h_bank = t_psum.tile([P, 512], F32, name="h_bank", tag="bank")
+                    for i in range(per_bank):
+                        for u in range(2):
+                            slot = 2 * i + u
+                            nc.tensor.transpose(
+                                h_bank[:, P * slot : P * (slot + 1)], words[:, first + i, u, :], ident_f32[:]
+                            )
+                    nc.scalar.copy(
+                        out=grouped_words[:, 256 * first : 256 * (first + per_bank)].rearrange(
+                            "q (g t u) -> q g t u", g=per_bank, u=2
+                        ),
+                        in_=h_bank[:].rearrange("q (g u t) -> q g t u", g=per_bank, u=2),
                     )
-            nc.vector.quantize_mx(out=h_codes[:].bitcast(FP8X4), scales=h_scales[:], in_=h_grouped[:])
+            for tt in range(TOKEN_TILES):
+                half = slice(PASSES * P * tt, PASSES * P * (tt + 1))
+                nc.vector.quantize_mx(
+                    out=h_codes[:, half].bitcast(FP8X4), scales=h_scales[:, half],
+                    in_=h_grouped[:, D * tt : D * (tt + 1)],
+                )
 
         raw_of = {}
+        split_of = {}
         grouped_of = {}
         codes_of = {}
         result_of = {}
@@ -158,13 +198,30 @@ def tile_attention_pa_kernel(tc, x, w_ln, wq, wk, wv, cos, sin, out_0, out_1, ou
             which, pair = units[n]
             rows = weights[which][UNIT_F * pair : UNIT_F * (pair + 1), :]
             w_raw = raw_pool.tile([P, 2 * D], BF16, name="w_raw")
-            nc.sync.dma_start(
-                out=w_raw[:].rearrange("p (n k) -> p n k", n=UNIT_HEADS), in_=rows.rearrange("(n p) k -> p n k", p=P)
-            )
+            raw_rows = w_raw[:].rearrange("p (n k) -> p n k", n=UNIT_HEADS)
+            pieces = 2 if n == 0 else 1
+            for i in range(pieces):
+                cols = slice(D // pieces * i, D // pieces * (i + 1))
+                nc.sync.dma_start(out=raw_rows[:, :, cols], in_=rows.rearrange("(n p) k -> p n k", p=P)[:, :, cols])
             raw_of[n] = w_raw
 
+        def split_unit(n):
+            who = splitter(n)
+            if who is None:
+                return
+            split = split_pool.tile([P, WORDS], F32, name="split")
+            copy = nc.vector.tensor_copy if who == "vector" else nc.scalar.copy
+            copy(
+                out=split[:].rearrange("f (c u q) -> f c u q", u=2, q=P),
+                in_=raw_of.pop(n)[:].bitcast(F32).rearrange("f (c q u) -> f c u q", u=2, q=P),
+            )
+            split_of[n] = split
+
         def transpose_unit(n):
-            words = raw_of.pop(n)[:].bitcast(F32).rearrange("f (n g q u) -> f n g u q", n=UNIT_HEADS, q=P, u=2)
+            if splitter(n) is None:
+                words = raw_of.pop(n)[:].bitcast(F32).rearrange("f (n g q u) -> f n g u q", n=UNIT_HEADS, q=P, u=2)
+            else:
+                words = split_of.pop(n)[:].rearrange("f (n g u q) -> f n g u q", n=UNIT_HEADS, q=P, u=2)
             grouped = grouped_pool.tile([P, PASSES * UNIT_F * PACK], BF16, name="grouped", align_bytes=64)
             grouped_words = grouped[:].bitcast(F32)
             for g in range(PASSES):
@@ -193,7 +250,8 @@ def tile_attention_pa_kernel(tc, x, w_ln, wq, wk, wv, cos, sin, out_0, out_1, ou
             acc = acc_psum.tile([P, TOKEN_TILES * UNIT_F], F32, name="acc")
             for tt in range(TOKEN_TILES):
                 for g in range(PASSES):
-                    tokens = slice(T * g + P * tt, T * g + P * (tt + 1))
+                    first = P * (PASSES * tt + g)
+                    tokens = slice(first, first + P)
                     feats = slice(UNIT_F * g, UNIT_F * (g + 1))
                     nc.tensor.matmul_mx(
                         out=acc[:, UNIT_F * tt : UNIT_F * (tt + 1)],
@@ -235,19 +293,26 @@ def tile_attention_pa_kernel(tc, x, w_ln, wq, wk, wv, cos, sin, out_0, out_1, ou
 
         for n in range(PREFETCH):
             load_unit(n)
-        rounds = UNITS // ROUND
-        for r in range(rounds + LAG):
-            if r < rounds:
-                for i in range(ROUND):
-                    transpose_unit(ROUND * r + i)
-            if r == H_ROUND:
+        make_h()
+        for n in range(AHEAD):
+            transpose_unit(n)
+            if n == 2:
                 quantise_h()
-            for i in range(ROUND):
-                if r >= LAG:
-                    multiply_unit(ROUND * (r - LAG) + i)
-                if r < rounds:
-                    quantise_unit(ROUND * r + i)
-                if r >= LAG:
-                    finish_unit(ROUND * (r - LAG) + i)
-                if ROUND * r + i + PREFETCH < UNITS:
-                    load_unit(ROUND * r + i + PREFETCH)
+            if n < 2:
+                quantise_unit(n)
+            load_unit(n + PREFETCH)
+        for n in range(0, UNITS, 2):
+            for i in (n + AHEAD + 2, n + AHEAD + 3):
+                if i < UNITS:
+                    split_unit(i)
+            for i in (n, n + 1):
+                if i + 2 < UNITS:
+                    quantise_unit(i + 2)
+                multiply_unit(i)
+            for i in (n, n + 1):
+                finish_unit(i)
+            for i in (n + AHEAD, n + AHEAD + 1):
+                if i < UNITS:
+                    transpose_unit(i)
+                    if i + PREFETCH < UNITS:
+                        load_unit(i + PREFETCH)

@@ -32,7 +32,7 @@ ACC_BANKS = 2
 T_BANKS = PSUM_BANKS - ACC_BANKS
 PREFETCH = 7
 RAW_BUFS = PREFETCH + 2
-SPLIT_BUFS = 4
+SPLIT_BUFS = 3
 GROUPED_BUFS = 3
 RES_BUFS = 6
 CODE_BUFS = 6
@@ -301,18 +301,14 @@ def tile_attention_pa_kernel(tc, x, w_ln, wq, wk, wv, cos, sin, out_0, out_1, ou
             if n < 2:
                 quantise_unit(n)
             load_unit(n + PREFETCH)
-        for n in range(0, UNITS, 2):
-            for i in (n + AHEAD + 2, n + AHEAD + 3):
-                if i < UNITS:
-                    split_unit(i)
-            for i in (n, n + 1):
-                if i + 2 < UNITS:
-                    quantise_unit(i + 2)
-                multiply_unit(i)
-            for i in (n, n + 1):
-                finish_unit(i)
-            for i in (n + AHEAD, n + AHEAD + 1):
-                if i < UNITS:
-                    transpose_unit(i)
-                    if i + PREFETCH < UNITS:
-                        load_unit(i + PREFETCH)
+        for i in range(UNITS):
+            multiply_unit(i)
+            if i + 2 < UNITS:
+                quantise_unit(i + 2)
+            finish_unit(i)
+            if i + AHEAD + 2 < UNITS:
+                split_unit(i + AHEAD + 2)
+            if i + AHEAD < UNITS:
+                transpose_unit(i + AHEAD)
+            if i + AHEAD + PREFETCH < UNITS:
+                load_unit(i + AHEAD + PREFETCH)

@@ -9,6 +9,7 @@ I32 = mybir.dt.int32
 U32 = mybir.dt.uint32
 U8 = mybir.dt.uint8
 FP8X4 = mybir.dt.float8_e4m3fn_x4
+ALU = mybir.AluOpType
 MULT = mybir.AluOpType.mult
 ADD = mybir.AluOpType.add
 ACT = mybir.ActivationFunctionType
@@ -36,6 +37,7 @@ SPLIT_BUFS = 3
 GROUPED_BUFS = 3
 RES_BUFS = 6
 CODE_BUFS = 6
+V_LAG = 2
 AHEAD = 4
 
 FLOPS = 2 * T * D * 3 * D
@@ -46,9 +48,9 @@ def unit_order():
     order = []
     for pair in range(pairs):
         order.extend([(0, pair), (1, pair)])
-        if pair > 0:
-            order.append((2, pair - 1))
-    order.append((2, pairs - 1))
+        if pair >= V_LAG:
+            order.append((2, pair - V_LAG))
+    order.extend([(2, pair) for pair in range(pairs - V_LAG, pairs)])
     return order
 
 
@@ -71,6 +73,7 @@ def tile_attention_pa_kernel(tc, x, w_ln, wq, wk, wv, cos, sin, out_0, out_1, ou
         grouped_pool = ctx.enter_context(tc.tile_pool(name="grouped", bufs=GROUPED_BUFS))
         code_pool = ctx.enter_context(tc.tile_pool(name="codes", bufs=CODE_BUFS))
         res_pool = ctx.enter_context(tc.tile_pool(name="res", bufs=RES_BUFS))
+        squares_pool = ctx.enter_context(tc.tile_pool(name="squares", bufs=1))
         far_pool = ctx.enter_context(tc.tile_pool(name="far", bufs=2))
         t_psum = ctx.enter_context(tc.psum_pool(name="t_psum", bufs=T_BANKS))
         acc_psum = ctx.enter_context(tc.psum_pool(name="acc_psum", bufs=ACC_BANKS))
@@ -79,14 +82,15 @@ def tile_attention_pa_kernel(tc, x, w_ln, wq, wk, wv, cos, sin, out_0, out_1, ou
         x_sb = []
         for tt in range(TOKEN_TILES):
             x_tile = keep.tile([P, D], BF16, name="x_sb%d" % tt)
-            nc.sync.dma_start(out=x_tile[:], in_=x_rows[:, tt, :])
             x_sb.append(x_tile)
+        nc.sync.dma_start(out=x_sb[0][:], in_=x_rows[:, 0, :])
 
         w_row = keep.tile([P, D], BF16, name="w_row")
         nc.vector.memset(w_row[:].bitcast(I32), 0)
         ones = keep.tile([P, P], BF16, name="ones")
         nc.vector.memset(ones[:], 1.0)
         nc.sync.dma_start(out=w_row[0:1, :], in_=w_ln.rearrange("(o k) -> o k", o=1))
+        nc.sync.dma_start(out=x_sb[1][:], in_=x_rows[:, 1, :])
         cos_sb = keep.tile([P, TOKEN_TILES * DH], BF16, name="cos_sb")
         nc.scalar.dma_start(out=cos_sb[:], in_=cos.rearrange("(p two) f -> p (two f)", two=TOKEN_TILES))
         sin_sb = keep.tile([P, TOKEN_TILES * DH], BF16, name="sin_sb")
@@ -108,7 +112,9 @@ def tile_attention_pa_kernel(tc, x, w_ln, wq, wk, wv, cos, sin, out_0, out_1, ou
         sin_heads = swap_view.unsqueeze(2).to_broadcast(table_shape)
 
         warm = keep.tile([P, 1], F32, name="warm")
-        nc.scalar.activation(out=warm[:], in_=ones[:, 0:1], func=ACT.Sqrt)
+        nc.scalar.activation(out=warm[:], in_=ones[:, 0:1], func=ACT.Square)
+        minus_half = keep.tile([P, TOKEN_TILES], F32, name="minus_half")
+        nc.gpsimd.memset(minus_half[:], -0.5)
 
         w_cols = D // ACC_BANKS
         w_all = []
@@ -128,38 +134,27 @@ def tile_attention_pa_kernel(tc, x, w_ln, wq, wk, wv, cos, sin, out_0, out_1, ou
         h_scales = keep.tile([P, TOKEN_TILES * PASSES * P], U8, name="h_scales", align_bytes=64)
 
         def make_h():
-            squares = keep.tile([P, D], BF16, name="squares")
-            sum_sq = keep.tile([P, 1], F32, name="sum_sq")
-            nc.scalar.activation(out=squares[:], in_=x_sb[0][:], func=ACT.Square, accum_out=sum_sq[:])
-            chunks = D // 512
-            stats = keep.tile([P, chunks * 6], F32, name="stats")
-            for c in range(chunks):
-                nc.vector.bn_stats(out=stats[:, 6 * c : 6 * (c + 1)], in_=x_sb[1][:, 512 * c : 512 * (c + 1)])
-            mean_var = keep.tile([P, 2], F32, name="mean_var")
-            nc.vector.bn_aggr(out=mean_var[:], in_=stats[:])
-            mean_sq = keep.tile([P, TOKEN_TILES], F32, name="mean_sq")
-            nc.vector.tensor_scalar(
-                out=mean_sq[:, 0:1], in0=sum_sq[:], scalar1=1.0 / D, scalar2=EPS, op0=MULT, op1=ADD
-            )
-            power = keep.tile([P, 1], F32, name="power")
-            nc.vector.scalar_tensor_tensor(
-                out=power[:], in0=mean_var[:, 0:1], scalar=mean_var[:, 0:1], in1=mean_var[:, 1:2], op0=MULT, op1=ADD,
-            )
-            nc.vector.tensor_scalar(
-                out=mean_sq[:, 1:2], in0=power[:], scalar1=1.0, scalar2=EPS, op0=MULT, op1=ADD
-            )
-            rms = keep.tile([P, TOKEN_TILES], F32, name="rms")
-            nc.scalar.activation(out=rms[:], in_=mean_sq[:], func=ACT.Sqrt)
-            r_cols = keep.tile([P, TOKEN_TILES], F32, name="r_cols")
-            nc.vector.reciprocal(out=r_cols[:], in_=rms[:])
+            sum_sq = keep.tile([P, TOKEN_TILES], F32, name="sum_sq")
+            xw = []
             for tt in range(TOKEN_TILES):
-                h_tile = keep.tile([P, D], BF16, name="h_bf%d" % tt)
+                squares = squares_pool.tile([P, D], BF16, name="squares")
+                nc.scalar.activation(
+                    out=squares[:], in_=x_sb[tt][:], func=ACT.Square, accum_out=sum_sq[:, tt : tt + 1]
+                )
+                xw_tile = keep.tile([P, D], F32, name="xw%d" % tt)
                 for b in range(ACC_BANKS):
                     cols = slice(w_cols * b, w_cols * (b + 1))
-                    nc.vector.scalar_tensor_tensor(
-                        out=h_tile[:, cols], in0=x_sb[tt][:, cols], scalar=r_cols[:, tt : tt + 1], in1=w_all[b][:],
-                        op0=MULT, op1=MULT,
-                    )
+                    nc.vector.tensor_tensor(out=xw_tile[:, cols], in0=x_sb[tt][:, cols], in1=w_all[b][:], op=MULT)
+                xw.append(xw_tile)
+            mean_sq = keep.tile([P, TOKEN_TILES], F32, name="mean_sq")
+            nc.vector.tensor_scalar(out=mean_sq[:], in0=sum_sq[:], scalar1=1.0 / D, scalar2=EPS, op0=MULT, op1=ADD)
+            r_cols = keep.tile([P, TOKEN_TILES], F32, name="r_cols")
+            nc.gpsimd.tensor_tensor(out=r_cols[:], in0=mean_sq[:], in1=minus_half[:], op=ALU.pow)
+            for tt in range(TOKEN_TILES):
+                h_tile = keep.tile([P, D], BF16, name="h_bf%d" % tt)
+                nc.vector.tensor_scalar(
+                    out=h_tile[:], in0=xw[tt][:], scalar1=r_cols[:, tt : tt + 1], scalar2=0.0, op0=MULT, op1=ADD,
+                )
                 h_bf.append(h_tile)
 
         def quantise_h():
@@ -175,7 +170,7 @@ def tile_attention_pa_kernel(tc, x, w_ln, wq, wk, wv, cos, sin, out_0, out_1, ou
                             nc.tensor.transpose(
                                 h_bank[:, P * slot : P * (slot + 1)], words[:, first + i, u, :], ident_f32[:]
                             )
-                    nc.scalar.copy(
+                    nc.vector.tensor_copy(
                         out=grouped_words[:, 256 * first : 256 * (first + per_bank)].rearrange(
                             "q (g t u) -> q g t u", g=per_bank, u=2
                         ),
@@ -241,7 +236,8 @@ def tile_attention_pa_kernel(tc, x, w_ln, wq, wk, wv, cos, sin, out_0, out_1, ou
         def quantise_unit(n):
             codes = code_pool.tile([P, PASSES * UNIT_F], U32, name="codes", align_bytes=64)
             scales = code_pool.tile([P, PASSES * UNIT_F], U8, name="scales", align_bytes=64)
-            nc.vector.quantize_mx(out=codes[:].bitcast(FP8X4), scales=scales[:], in_=grouped_of.pop(n)[:])
+            grouped = grouped_of.pop(n)
+            nc.vector.quantize_mx(out=codes[:].bitcast(FP8X4), scales=scales[:], in_=grouped[:])
             codes_of[n] = (codes, scales)
 
         def multiply_unit(n):
@@ -275,16 +271,42 @@ def tile_attention_pa_kernel(tc, x, w_ln, wq, wk, wv, cos, sin, out_0, out_1, ou
                 nc.vector.tensor_tensor(out=far_view, in0=acc_view, in1=sin_heads, op=MULT)
                 result_of[n] = (res, far)
 
+        def multiply_last_unit(n):
+            which, pair = units[n]
+            codes, scales = codes_of.pop(n)
+            accs = [
+                acc_psum.tile([P, UNIT_F], F32, name="acc_0", tag="acc"),
+                t_psum.tile([P, UNIT_F], F32, name="acc_1", tag="bank"),
+            ]
+            for g in range(PASSES):
+                for tt in range(TOKEN_TILES):
+                    first = P * (PASSES * tt + g)
+                    tokens = slice(first, first + P)
+                    feats = slice(UNIT_F * g, UNIT_F * (g + 1))
+                    nc.tensor.matmul_mx(
+                        out=accs[tt][:],
+                        lhsT=h_codes[:, tokens].bitcast(FP8X4),
+                        lhsT_scale=h_scales[:, tokens],
+                        rhs=codes[:, feats].bitcast(FP8X4),
+                        rhs_scale=scales[:, feats],
+                        start=(g == 0),
+                        stop=(g == PASSES - 1),
+                    )
+            heads = outs[which][UNIT_HEADS * pair : UNIT_HEADS * (pair + 1), :, :]
+            rows = heads.rearrange("h (p t) f -> p t h f", t=TOKEN_TILES)
+            for tt in range(TOKEN_TILES):
+                res = res_pool.tile([P, UNIT_F], F32, name="res_last%d" % tt, tag="res")
+                copy = nc.scalar.copy if tt == 0 else nc.vector.tensor_copy
+                copy(out=res[:], in_=accs[tt][:])
+                nc.sync.dma_start(out=rows[:, tt, :, :], in_=res[:].rearrange("p (h f) -> p h f", h=UNIT_HEADS))
+
         def finish_unit(n):
             which, pair = units[n]
             res, far = result_of.pop(n)
             if far is not None:
                 res_halves = res[:].rearrange("p (c s j) -> p c s j", s=2, j=HALF)
                 far_halves = far[:].rearrange("p (c s j) -> p c s j", s=2, j=HALF)
-                for s in range(2):
-                    nc.vector.tensor_tensor(
-                        out=res_halves[:, :, s, :], in0=res_halves[:, :, s, :], in1=far_halves[:, :, 1 - s, :], op=ADD,
-                    )
+                nc.vector.tensor_tensor(out=res_halves, in0=res_halves, in1=far_halves[:, :, ::-1, :], op=ADD)
             heads = outs[which][UNIT_HEADS * pair : UNIT_HEADS * (pair + 1), :, :]
             nc.sync.dma_start(
                 out=heads.rearrange("h (p t) f -> p h (t f)", t=TOKEN_TILES),
@@ -296,19 +318,22 @@ def tile_attention_pa_kernel(tc, x, w_ln, wq, wk, wv, cos, sin, out_0, out_1, ou
         make_h()
         for n in range(AHEAD):
             transpose_unit(n)
-            if n == 2:
+            if n == 1:
                 quantise_h()
             if n < 2:
                 quantise_unit(n)
             load_unit(n + PREFETCH)
-        for i in range(UNITS):
-            multiply_unit(i)
+        for i in range(UNITS - 1):
             if i + 2 < UNITS:
                 quantise_unit(i + 2)
-            finish_unit(i)
+            multiply_unit(i)
+            if i > 0:
+                finish_unit(i - 1)
             if i + AHEAD + 2 < UNITS:
                 split_unit(i + AHEAD + 2)
             if i + AHEAD < UNITS:
                 transpose_unit(i + AHEAD)
             if i + AHEAD + PREFETCH < UNITS:
                 load_unit(i + AHEAD + PREFETCH)
+        finish_unit(UNITS - 2)
+        multiply_last_unit(UNITS - 1)

@@ -55,7 +55,7 @@ def unit_order():
 
 
 def splitter(n):
-    if n < 2 * AHEAD or n % 3 == 0:
+    if n < AHEAD + 2 or n % 3 == 1:
         return None
     return "scalar" if n % 4 == 0 else "vector"
 
@@ -74,7 +74,7 @@ def tile_attention_pa_kernel(tc, x, w_ln, wq, wk, wv, cos, sin, out_0, out_1, ou
         code_pool = ctx.enter_context(tc.tile_pool(name="codes", bufs=CODE_BUFS))
         res_pool = ctx.enter_context(tc.tile_pool(name="res", bufs=RES_BUFS))
         squares_pool = ctx.enter_context(tc.tile_pool(name="squares", bufs=1))
-        far_pool = ctx.enter_context(tc.tile_pool(name="far", bufs=2))
+        terms_pool = ctx.enter_context(tc.tile_pool(name="terms", bufs=2))
         t_psum = ctx.enter_context(tc.psum_pool(name="t_psum", bufs=T_BANKS))
         acc_psum = ctx.enter_context(tc.psum_pool(name="acc_psum", bufs=ACC_BANKS))
 
@@ -99,21 +99,9 @@ def tile_attention_pa_kernel(tc, x, w_ln, wq, wk, wv, cos, sin, out_0, out_1, ou
         ident_f32 = keep.tile([P, P], F32, name="ident_f32")
         make_identity(nc, ident_f32[:])
 
-        sin_swap = keep.tile([P, TOKEN_TILES * DH], BF16, name="sin_swap")
-        sin_view = sin_sb[:].rearrange("p (t f) -> p t f", t=TOKEN_TILES)
-        swap_view = sin_swap[:].rearrange("p (t f) -> p t f", t=TOKEN_TILES)
-        nc.gpsimd.tensor_copy(out=swap_view[:, :, 0:HALF], in_=sin_view[:, :, HALF:DH])
-        nc.gpsimd.tensor_scalar(
-            out=swap_view[:, :, HALF:DH], in0=sin_view[:, :, 0:HALF],
-            scalar1=-1.0, scalar2=0.0, op0=MULT, op1=ADD,
-        )
-        table_shape = [P, TOKEN_TILES, UNIT_HEADS, DH]
-        cos_heads = cos_sb[:].rearrange("p (t f) -> p t f", t=TOKEN_TILES).unsqueeze(2).to_broadcast(table_shape)
-        sin_heads = swap_view.unsqueeze(2).to_broadcast(table_shape)
-
         warm = keep.tile([P, 1], F32, name="warm")
         nc.scalar.activation(out=warm[:], in_=ones[:, 0:1], func=ACT.Square)
-        minus_half = keep.tile([P, TOKEN_TILES], F32, name="minus_half")
+        minus_half = keep.tile([P, 1], F32, name="minus_half")
         nc.gpsimd.memset(minus_half[:], -0.5)
 
         w_cols = D // ACC_BANKS
@@ -133,54 +121,60 @@ def tile_attention_pa_kernel(tc, x, w_ln, wq, wk, wv, cos, sin, out_0, out_1, ou
         h_codes = keep.tile([P, TOKEN_TILES * PASSES * P], U32, name="h_codes", align_bytes=64)
         h_scales = keep.tile([P, TOKEN_TILES * PASSES * P], U8, name="h_scales", align_bytes=64)
 
-        def make_h():
-            sum_sq = keep.tile([P, TOKEN_TILES], F32, name="sum_sq")
-            xw = []
-            for tt in range(TOKEN_TILES):
-                squares = squares_pool.tile([P, D], BF16, name="squares")
-                nc.scalar.activation(
-                    out=squares[:], in_=x_sb[tt][:], func=ACT.Square, accum_out=sum_sq[:, tt : tt + 1]
+        def make_h(tt):
+            squares = squares_pool.tile([P, D], BF16, name="squares")
+            sum_sq = keep.tile([P, 1], F32, name="sum_sq%d" % tt)
+            nc.scalar.activation(out=squares[:], in_=x_sb[tt][:], func=ACT.Square, accum_out=sum_sq[:])
+            mean_sq = keep.tile([P, 1], F32, name="mean_sq%d" % tt)
+            nc.gpsimd.tensor_scalar(out=mean_sq[:], in0=sum_sq[:], scalar1=1.0 / D, scalar2=EPS, op0=MULT, op1=ADD)
+            r_col = keep.tile([P, 1], F32, name="r_col%d" % tt)
+            nc.gpsimd.tensor_tensor(out=r_col[:], in0=mean_sq[:], in1=minus_half[:], op=ALU.pow)
+            h_tile = keep.tile([P, D], BF16, name="h_bf%d" % tt)
+            for b in range(ACC_BANKS):
+                cols = slice(w_cols * b, w_cols * (b + 1))
+                nc.vector.scalar_tensor_tensor(
+                    out=h_tile[:, cols], in0=x_sb[tt][:, cols], scalar=r_col[:], in1=w_all[b][:], op0=MULT, op1=MULT,
                 )
-                xw_tile = keep.tile([P, D], F32, name="xw%d" % tt)
-                for b in range(ACC_BANKS):
-                    cols = slice(w_cols * b, w_cols * (b + 1))
-                    nc.vector.tensor_tensor(out=xw_tile[:, cols], in0=x_sb[tt][:, cols], in1=w_all[b][:], op=MULT)
-                xw.append(xw_tile)
-            mean_sq = keep.tile([P, TOKEN_TILES], F32, name="mean_sq")
-            nc.vector.tensor_scalar(out=mean_sq[:], in0=sum_sq[:], scalar1=1.0 / D, scalar2=EPS, op0=MULT, op1=ADD)
-            r_cols = keep.tile([P, TOKEN_TILES], F32, name="r_cols")
-            nc.gpsimd.tensor_tensor(out=r_cols[:], in0=mean_sq[:], in1=minus_half[:], op=ALU.pow)
-            for tt in range(TOKEN_TILES):
-                h_tile = keep.tile([P, D], BF16, name="h_bf%d" % tt)
-                nc.vector.tensor_scalar(
-                    out=h_tile[:], in0=xw[tt][:], scalar1=r_cols[:, tt : tt + 1], scalar2=0.0, op0=MULT, op1=ADD,
-                )
-                h_bf.append(h_tile)
+            h_bf.append(h_tile)
 
-        def quantise_h():
-            for tt in range(TOKEN_TILES):
-                words = h_bf[tt][:].bitcast(F32).rearrange("t (g q u) -> t g u q", q=P, u=2)
-                grouped_words = h_grouped[:, D * tt : D * (tt + 1)].bitcast(F32)
-                per_bank = 2
-                for first in range(0, PASSES, per_bank):
-                    h_bank = t_psum.tile([P, 512], F32, name="h_bank", tag="bank")
-                    for i in range(per_bank):
-                        for u in range(2):
-                            slot = 2 * i + u
-                            nc.tensor.transpose(
-                                h_bank[:, P * slot : P * (slot + 1)], words[:, first + i, u, :], ident_f32[:]
-                            )
-                    nc.vector.tensor_copy(
-                        out=grouped_words[:, 256 * first : 256 * (first + per_bank)].rearrange(
-                            "q (g t u) -> q g t u", g=per_bank, u=2
-                        ),
-                        in_=h_bank[:].rearrange("q (g u t) -> q g t u", g=per_bank, u=2),
-                    )
-            for tt in range(TOKEN_TILES):
-                half = slice(PASSES * P * tt, PASSES * P * (tt + 1))
-                nc.vector.quantize_mx(
-                    out=h_codes[:, half].bitcast(FP8X4), scales=h_scales[:, half],
-                    in_=h_grouped[:, D * tt : D * (tt + 1)],
+        def transpose_h(tt):
+            words = h_bf[tt][:].bitcast(F32).rearrange("t (g q u) -> t g u q", q=P, u=2)
+            grouped_words = h_grouped[:, D * tt : D * (tt + 1)].bitcast(F32)
+            per_bank = 2
+            for first in range(0, PASSES, per_bank):
+                h_bank = t_psum.tile([P, 512], F32, name="h_bank", tag="bank")
+                for i in range(per_bank):
+                    for u in range(2):
+                        slot = 2 * i + u
+                        nc.tensor.transpose(
+                            h_bank[:, P * slot : P * (slot + 1)], words[:, first + i, u, :], ident_f32[:]
+                        )
+                nc.vector.tensor_copy(
+                    out=grouped_words[:, 256 * first : 256 * (first + per_bank)].rearrange(
+                        "q (g t u) -> q g t u", g=per_bank, u=2
+                    ),
+                    in_=h_bank[:].rearrange("q (g u t) -> q g t u", g=per_bank, u=2),
+                )
+
+        def quantise_h(tt):
+            half = slice(PASSES * P * tt, PASSES * P * (tt + 1))
+            nc.vector.quantize_mx(
+                out=h_codes[:, half].bitcast(FP8X4), scales=h_scales[:, half],
+                in_=h_grouped[:, D * tt : D * (tt + 1)],
+            )
+
+        tables = keep.tile([P, 2 * TOKEN_TILES * UNIT_F], BF16, name="tables")
+
+        def make_tables():
+            view = tables[:].rearrange("p (w t h f) -> p w t h f", w=2, t=TOKEN_TILES, h=UNIT_HEADS)
+            cos_view = cos_sb[:].rearrange("p (t f) -> p t f", t=TOKEN_TILES)
+            sin_view = sin_sb[:].rearrange("p (t f) -> p t f", t=TOKEN_TILES)
+            for head in range(UNIT_HEADS):
+                nc.vector.tensor_copy(out=view[:, 0, :, head, :], in_=cos_view)
+                nc.vector.tensor_copy(out=view[:, 1, :, head, 0:HALF], in_=sin_view[:, :, HALF:DH])
+                nc.vector.tensor_scalar(
+                    out=view[:, 1, :, head, HALF:DH], in0=sin_view[:, :, 0:HALF],
+                    scalar1=-1.0, scalar2=0.0, op0=MULT, op1=ADD,
                 )
 
         raw_of = {}
@@ -258,18 +252,21 @@ def tile_attention_pa_kernel(tc, x, w_ln, wq, wk, wv, cos, sin, out_0, out_1, ou
                         start=(g == 0),
                         stop=(g == PASSES - 1),
                     )
-            acc_view = acc[:].rearrange("p (t h f) -> p t h f", t=TOKEN_TILES, h=UNIT_HEADS)
             res = res_pool.tile([P, TOKEN_TILES * UNIT_F], F32, name="res")
-            res_view = res[:].rearrange("p (h t f) -> p t h f", h=UNIT_HEADS, t=TOKEN_TILES)
             if which == 2:
-                nc.scalar.copy(out=res_view, in_=acc_view)
+                nc.scalar.copy(
+                    out=res[:].rearrange("p (h t f) -> p t h f", h=UNIT_HEADS, t=TOKEN_TILES),
+                    in_=acc[:].rearrange("p (t h f) -> p t h f", t=TOKEN_TILES, h=UNIT_HEADS),
+                )
                 result_of[n] = (res, None)
             else:
-                far = far_pool.tile([P, TOKEN_TILES * UNIT_F], F32, name="far")
-                far_view = far[:].rearrange("p (h t f) -> p t h f", h=UNIT_HEADS, t=TOKEN_TILES)
-                nc.vector.tensor_tensor(out=res_view, in0=acc_view, in1=cos_heads, op=MULT)
-                nc.vector.tensor_tensor(out=far_view, in0=acc_view, in1=sin_heads, op=MULT)
-                result_of[n] = (res, far)
+                both = [P, 2, TOKEN_TILES * UNIT_F]
+                terms = terms_pool.tile(both, F32, name="terms")
+                nc.vector.tensor_tensor(
+                    out=terms[:], in0=acc[:].unsqueeze(1).to_broadcast(both),
+                    in1=tables[:].rearrange("p (w c) -> p w c", w=2), op=MULT,
+                )
+                result_of[n] = (res, terms)
 
         def multiply_last_unit(n):
             which, pair = units[n]
@@ -302,11 +299,14 @@ def tile_attention_pa_kernel(tc, x, w_ln, wq, wk, wv, cos, sin, out_0, out_1, ou
 
         def finish_unit(n):
             which, pair = units[n]
-            res, far = result_of.pop(n)
-            if far is not None:
-                res_halves = res[:].rearrange("p (c s j) -> p c s j", s=2, j=HALF)
-                far_halves = far[:].rearrange("p (c s j) -> p c s j", s=2, j=HALF)
-                nc.vector.tensor_tensor(out=res_halves, in0=res_halves, in1=far_halves[:, :, ::-1, :], op=ADD)
+            res, terms = result_of.pop(n)
+            if terms is not None:
+                near = terms[:, 0, :].rearrange("p (t h s j) -> p t h s j", t=TOKEN_TILES, h=UNIT_HEADS, s=2)
+                far = terms[:, 1, :].rearrange("p (t h s j) -> p t h s j", t=TOKEN_TILES, h=UNIT_HEADS, s=2)
+                nc.vector.tensor_tensor(
+                    out=res[:].rearrange("p (h t s j) -> p t h s j", t=TOKEN_TILES, h=UNIT_HEADS, s=2),
+                    in0=near, in1=far[:, :, :, ::-1, :], op=ADD,
+                )
             heads = outs[which][UNIT_HEADS * pair : UNIT_HEADS * (pair + 1), :, :]
             nc.sync.dma_start(
                 out=heads.rearrange("h (p t) f -> p h (t f)", t=TOKEN_TILES),
@@ -315,13 +315,15 @@ def tile_attention_pa_kernel(tc, x, w_ln, wq, wk, wv, cos, sin, out_0, out_1, ou
 
         for n in range(PREFETCH):
             load_unit(n)
-        make_h()
+        make_tables()
+        for tt in range(TOKEN_TILES):
+            make_h(tt)
         for n in range(AHEAD):
             transpose_unit(n)
-            if n == 1:
-                quantise_h()
-            if n < 2:
+            if n < TOKEN_TILES:
+                transpose_h(n)
                 quantise_unit(n)
+                quantise_h(n)
             load_unit(n + PREFETCH)
         for i in range(UNITS - 1):
             if i + 2 < UNITS:

@@ -111,15 +111,24 @@ def tile_attention_pa_kernel(tc, x, w_ln, wq, wk, wv, cos, sin, out_0, out_1, ou
             for c in range(w_cols // 512):
                 first = w_cols * b + 512 * c
                 nc.tensor.matmul(
-                    out=w_bank[:, 512 * c : 512 * (c + 1)], lhsT=ones[:], rhs=w_row[:, first : first + 512],
+                    out=w_bank[:, 512 * c : 512 * (c + 1)].rearrange("p (u q e) -> p u q e", u=2, q=P),
+                    lhsT=ones[:], rhs=w_row[:, first : first + 512].rearrange("p (q u e) -> p u q e", u=2, q=P),
                     start=True, stop=True,
                 )
             w_all.append(w_bank)
 
+        x_split = []
+        for tt in range(TOKEN_TILES):
+            x_apart = keep.tile([P, D], BF16, name="x_apart%d" % tt)
+            nc.vector.tensor_copy(
+                out=x_apart[:].bitcast(F32).rearrange("p (g u q) -> p g u q", u=2, q=P),
+                in_=x_sb[tt][:].bitcast(F32).rearrange("p (g q u) -> p g u q", u=2, q=P),
+            )
+            x_split.append(x_apart)
         h_bf = []
         h_grouped = keep.tile([P, TOKEN_TILES * PASSES * P * PACK], BF16, name="h_grouped", align_bytes=64)
-        h_codes = keep.tile([P, TOKEN_TILES * PASSES * P], U32, name="h_codes", align_bytes=64)
-        h_scales = keep.tile([P, TOKEN_TILES * PASSES * P], U8, name="h_scales", align_bytes=64)
+        h_codes = keep.tile([P, TOKEN_TILES * PASSES * P], U32, name="h_codes", align_bytes=256)
+        h_scales = keep.tile([P, TOKEN_TILES * PASSES * P], U8, name="h_scales", align_bytes=256)
 
         def make_h(tt):
             squares = squares_pool.tile([P, D], BF16, name="squares")
@@ -133,12 +142,12 @@ def tile_attention_pa_kernel(tc, x, w_ln, wq, wk, wv, cos, sin, out_0, out_1, ou
             for b in range(ACC_BANKS):
                 cols = slice(w_cols * b, w_cols * (b + 1))
                 nc.vector.scalar_tensor_tensor(
-                    out=h_tile[:, cols], in0=x_sb[tt][:, cols], scalar=r_col[:], in1=w_all[b][:], op0=MULT, op1=MULT,
+                    out=h_tile[:, cols], in0=x_split[tt][:, cols], scalar=r_col[:], in1=w_all[b][:], op0=MULT, op1=MULT,
                 )
             h_bf.append(h_tile)
 
         def transpose_h(tt):
-            words = h_bf[tt][:].bitcast(F32).rearrange("t (g q u) -> t g u q", q=P, u=2)
+            words = h_bf[tt][:].bitcast(F32).rearrange("t (g u q) -> t g u q", q=P, u=2)
             grouped_words = h_grouped[:, D * tt : D * (tt + 1)].bitcast(F32)
             per_bank = 2
             for first in range(0, PASSES, per_bank):
@@ -228,8 +237,8 @@ def tile_attention_pa_kernel(tc, x, w_ln, wq, wk, wv, cos, sin, out_0, out_1, ou
             grouped_of[n] = grouped
 
         def quantise_unit(n):
-            codes = code_pool.tile([P, PASSES * UNIT_F], U32, name="codes", align_bytes=64)
-            scales = code_pool.tile([P, PASSES * UNIT_F], U8, name="scales", align_bytes=64)
+            codes = code_pool.tile([P, PASSES * UNIT_F], U32, name="codes", align_bytes=256)
+            scales = code_pool.tile([P, PASSES * UNIT_F], U8, name="scales", align_bytes=256)
             grouped = grouped_of.pop(n)
             nc.vector.quantize_mx(out=codes[:].bitcast(FP8X4), scales=scales[:], in_=grouped[:])
             codes_of[n] = (codes, scales)

@@ -54,10 +54,8 @@ def unit_order():
     return order
 
 
-def splitter(n):
-    if n < AHEAD + 2 or n % 3 == 1:
-        return None
-    return "scalar" if n % 4 == 0 else "vector"
+def is_split(n):
+    return n >= AHEAD + 2 and n % 2 == 0
 
 
 def tile_attention_pa_kernel(tc, x, w_ln, wq, wk, wv, cos, sin, out_0, out_1, out_2):
@@ -204,22 +202,20 @@ def tile_attention_pa_kernel(tc, x, w_ln, wq, wk, wv, cos, sin, out_0, out_1, ou
             raw_of[n] = w_raw
 
         def split_unit(n):
-            who = splitter(n)
-            if who is None:
+            if not is_split(n):
                 return
             split = split_pool.tile([P, WORDS], F32, name="split")
-            copy = nc.vector.tensor_copy if who == "vector" else nc.scalar.copy
-            copy(
+            nc.vector.tensor_copy(
                 out=split[:].rearrange("f (c u q) -> f c u q", u=2, q=P),
                 in_=raw_of.pop(n)[:].bitcast(F32).rearrange("f (c q u) -> f c u q", u=2, q=P),
             )
             split_of[n] = split
 
         def transpose_unit(n):
-            if splitter(n) is None:
-                words = raw_of.pop(n)[:].bitcast(F32).rearrange("f (n g q u) -> f n g u q", n=UNIT_HEADS, q=P, u=2)
-            else:
+            if is_split(n):
                 words = split_of.pop(n)[:].rearrange("f (n g u q) -> f n g u q", n=UNIT_HEADS, q=P, u=2)
+            else:
+                words = raw_of.pop(n)[:].bitcast(F32).rearrange("f (n g q u) -> f n g u q", n=UNIT_HEADS, q=P, u=2)
             grouped = grouped_pool.tile([P, PASSES * UNIT_F * PACK], BF16, name="grouped", align_bytes=64)
             grouped_words = grouped[:].bitcast(F32)
             for g in range(PASSES):

from contextlib import ExitStack

import concourse.mybir as mybir
from concourse.masks import make_identity

F32 = mybir.dt.float32
BF16 = mybir.dt.bfloat16
I32 = mybir.dt.int32
U32 = mybir.dt.uint32
U8 = mybir.dt.uint8
FP8X4 = mybir.dt.float8_e4m3fn_x4
ALU = mybir.AluOpType
MULT = mybir.AluOpType.mult
ADD = mybir.AluOpType.add
ACT = mybir.ActivationFunctionType

P = 128
T, D, H, DH = 256, 2048, 16, 128
EPS = 1e-5
PACK = 4
K_PASS = P * PACK
PASSES = D // K_PASS
TOKEN_TILES = T // P
HALF = DH // 2

UNIT_HEADS = 2
UNIT_F = UNIT_HEADS * DH
UNITS = 3 * H // UNIT_HEADS
WORDS = UNIT_HEADS * D // 2

PSUM_BANKS = 8
ACC_BANKS = 2
T_BANKS = PSUM_BANKS - ACC_BANKS
PREFETCH = 7
RAW_BUFS = PREFETCH + 2
SPLIT_BUFS = 3
GROUPED_BUFS = 3
RES_BUFS = 6
CODE_BUFS = 6
V_LAG = 2
AHEAD = 4

FLOPS = 2 * T * D * 3 * D


def unit_order():
    pairs = H // UNIT_HEADS
    order = []
    for pair in range(pairs):
        order.extend([(0, pair), (1, pair)])
        if pair >= V_LAG:
            order.append((2, pair - V_LAG))
    order.extend([(2, pair) for pair in range(pairs - V_LAG, pairs)])
    return order


def is_split(n):
    return n >= AHEAD + 2 and n % 2 == 0


def tile_attention_pa_kernel(tc, x, w_ln, wq, wk, wv, cos, sin, out_0, out_1, out_2):
    nc = tc.nc
    weights = (wq, wk, wv)
    outs = (out_0, out_1, out_2)
    units = unit_order()
    with ExitStack() as ctx:
        ctx.enter_context(tc.manual_schedule())
        keep = ctx.enter_context(tc.tile_pool(name="keep", bufs=1))
        raw_pool = ctx.enter_context(tc.tile_pool(name="raw", bufs=RAW_BUFS))
        split_pool = ctx.enter_context(tc.tile_pool(name="split", bufs=SPLIT_BUFS))
        grouped_pool = ctx.enter_context(tc.tile_pool(name="grouped", bufs=GROUPED_BUFS))
        code_pool = ctx.enter_context(tc.tile_pool(name="codes", bufs=CODE_BUFS))
        res_pool = ctx.enter_context(tc.tile_pool(name="res", bufs=RES_BUFS))
        squares_pool = ctx.enter_context(tc.tile_pool(name="squares", bufs=1))
        terms_pool = ctx.enter_context(tc.tile_pool(name="terms", bufs=2))
        t_psum = ctx.enter_context(tc.psum_pool(name="t_psum", bufs=T_BANKS))
        acc_psum = ctx.enter_context(tc.psum_pool(name="acc_psum", bufs=ACC_BANKS))

        x_rows = x.rearrange("(p two) k -> p two k", two=TOKEN_TILES)
        x_sb = []
        for tt in range(TOKEN_TILES):
            x_tile = keep.tile([P, D], BF16, name="x_sb%d" % tt)
            x_sb.append(x_tile)
        nc.sync.dma_start(out=x_sb[0][:], in_=x_rows[:, 0, :])

        w_row = keep.tile([P, D], BF16, name="w_row")
        nc.vector.memset(w_row[:].bitcast(I32), 0)
        ones = keep.tile([P, P], BF16, name="ones")
        nc.vector.memset(ones[:], 1.0)
        nc.sync.dma_start(out=w_row[0:1, :], in_=w_ln.rearrange("(o k) -> o k", o=1))
        nc.sync.dma_start(out=x_sb[1][:], in_=x_rows[:, 1, :])
        cos_sb = keep.tile([P, TOKEN_TILES * DH], BF16, name="cos_sb")
        nc.scalar.dma_start(out=cos_sb[:], in_=cos.rearrange("(p two) f -> p (two f)", two=TOKEN_TILES))
        sin_sb = keep.tile([P, TOKEN_TILES * DH], BF16, name="sin_sb")
        nc.scalar.dma_start(out=sin_sb[:], in_=sin.rearrange("(p two) f -> p (two f)", two=TOKEN_TILES))

        ident_f32 = keep.tile([P, P], F32, name="ident_f32")
        make_identity(nc, ident_f32[:])

        warm = keep.tile([P, 1], F32, name="warm")
        nc.scalar.activation(out=warm[:], in_=ones[:, 0:1], func=ACT.Square)
        minus_half = keep.tile([P, 1], F32, name="minus_half")
        nc.gpsimd.memset(minus_half[:], -0.5)

        w_cols = D // ACC_BANKS
        w_all = []
        for b in range(ACC_BANKS):
            w_bank = acc_psum.tile([P, w_cols], BF16, name="w_bank", tag="acc")
            for c in range(w_cols // 512):
                first = w_cols * b + 512 * c
                nc.tensor.matmul(
                    out=w_bank[:, 512 * c : 512 * (c + 1)].rearrange("p (u q e) -> p u q e", u=2, q=P),
                    lhsT=ones[:], rhs=w_row[:, first : first + 512].rearrange("p (q u e) -> p u q e", u=2, q=P),
                    start=True, stop=True,
                )
            w_all.append(w_bank)

        x_split = []
        for tt in range(TOKEN_TILES):
            x_apart = keep.tile([P, D], BF16, name="x_apart%d" % tt)
            nc.vector.tensor_copy(
                out=x_apart[:].bitcast(F32).rearrange("p (g u q) -> p g u q", u=2, q=P),
                in_=x_sb[tt][:].bitcast(F32).rearrange("p (g q u) -> p g u q", u=2, q=P),
            )
            x_split.append(x_apart)
        h_bf = []
        h_grouped = keep.tile([P, TOKEN_TILES * PASSES * P * PACK], BF16, name="h_grouped", align_bytes=64)
        h_codes = keep.tile([P, TOKEN_TILES * PASSES * P], U32, name="h_codes", align_bytes=256)
        h_scales = keep.tile([P, TOKEN_TILES * PASSES * P], U8, name="h_scales", align_bytes=256)

        def make_h(tt):
            squares = squares_pool.tile([P, D], BF16, name="squares")
            sum_sq = keep.tile([P, 1], F32, name="sum_sq%d" % tt)
            nc.scalar.activation(out=squares[:], in_=x_sb[tt][:], func=ACT.Square, accum_out=sum_sq[:])
            mean_sq = keep.tile([P, 1], F32, name="mean_sq%d" % tt)
            nc.gpsimd.tensor_scalar(out=mean_sq[:], in0=sum_sq[:], scalar1=1.0 / D, scalar2=EPS, op0=MULT, op1=ADD)
            r_col = keep.tile([P, 1], F32, name="r_col%d" % tt)
            nc.gpsimd.tensor_tensor(out=r_col[:], in0=mean_sq[:], in1=minus_half[:], op=ALU.pow)
            h_tile = keep.tile([P, D], BF16, name="h_bf%d" % tt)
            for b in range(ACC_BANKS):
                cols = slice(w_cols * b, w_cols * (b + 1))
                nc.vector.scalar_tensor_tensor(
                    out=h_tile[:, cols], in0=x_split[tt][:, cols], scalar=r_col[:], in1=w_all[b][:], op0=MULT, op1=MULT,
                )
            h_bf.append(h_tile)

        def transpose_h(tt):
            words = h_bf[tt][:].bitcast(F32).rearrange("t (g u q) -> t g u q", q=P, u=2)
            grouped_words = h_grouped[:, D * tt : D * (tt + 1)].bitcast(F32)
            per_bank = 2
            for first in range(0, PASSES, per_bank):
                h_bank = t_psum.tile([P, 512], F32, name="h_bank", tag="bank")
                for i in range(per_bank):
                    for u in range(2):
                        slot = 2 * i + u
                        nc.tensor.transpose(
                            h_bank[:, P * slot : P * (slot + 1)], words[:, first + i, u, :], ident_f32[:]
                        )
                nc.vector.tensor_copy(
                    out=grouped_words[:, 256 * first : 256 * (first + per_bank)].rearrange(
                        "q (g t u) -> q g t u", g=per_bank, u=2
                    ),
                    in_=h_bank[:].rearrange("q (g u t) -> q g t u", g=per_bank, u=2),
                )

        def quantise_h(tt):
            half = slice(PASSES * P * tt, PASSES * P * (tt + 1))
            nc.vector.quantize_mx(
                out=h_codes[:, half].bitcast(FP8X4), scales=h_scales[:, half],
                in_=h_grouped[:, D * tt : D * (tt + 1)],
            )

        tables = keep.tile([P, 2 * TOKEN_TILES * UNIT_F], BF16, name="tables")

        def make_tables():
            view = tables[:].rearrange("p (w t h f) -> p w t h f", w=2, t=TOKEN_TILES, h=UNIT_HEADS)
            cos_view = cos_sb[:].rearrange("p (t f) -> p t f", t=TOKEN_TILES)
            sin_view = sin_sb[:].rearrange("p (t f) -> p t f", t=TOKEN_TILES)
            for head in range(UNIT_HEADS):
                nc.vector.tensor_copy(out=view[:, 0, :, head, :], in_=cos_view)
                nc.vector.tensor_copy(out=view[:, 1, :, head, 0:HALF], in_=sin_view[:, :, HALF:DH])
                nc.vector.tensor_scalar(
                    out=view[:, 1, :, head, HALF:DH], in0=sin_view[:, :, 0:HALF],
                    scalar1=-1.0, scalar2=0.0, op0=MULT, op1=ADD,
                )

        raw_of = {}
        split_of = {}
        grouped_of = {}
        codes_of = {}
        result_of = {}

        def load_unit(n):
            which, pair = units[n]
            rows = weights[which][UNIT_F * pair : UNIT_F * (pair + 1), :]
            w_raw = raw_pool.tile([P, 2 * D], BF16, name="w_raw")
            raw_rows = w_raw[:].rearrange("p (n k) -> p n k", n=UNIT_HEADS)
            pieces = 2 if n == 0 else 1
            for i in range(pieces):
                cols = slice(D // pieces * i, D // pieces * (i + 1))
                nc.sync.dma_start(out=raw_rows[:, :, cols], in_=rows.rearrange("(n p) k -> p n k", p=P)[:, :, cols])
            raw_of[n] = w_raw

        def split_unit(n):
            if not is_split(n):
                return
            split = split_pool.tile([P, WORDS], F32, name="split")
            nc.vector.tensor_copy(
                out=split[:].rearrange("f (c u q) -> f c u q", u=2, q=P),
                in_=raw_of.pop(n)[:].bitcast(F32).rearrange("f (c q u) -> f c u q", u=2, q=P),
            )
            split_of[n] = split

        def transpose_unit(n):
            if is_split(n):
                words = split_of.pop(n)[:].rearrange("f (n g u q) -> f n g u q", n=UNIT_HEADS, q=P, u=2)
            else:
                words = raw_of.pop(n)[:].bitcast(F32).rearrange("f (n g q u) -> f n g u q", n=UNIT_HEADS, q=P, u=2)
            grouped = grouped_pool.tile([P, PASSES * UNIT_F * PACK], BF16, name="grouped", align_bytes=64)
            grouped_words = grouped[:].bitcast(F32)
            for g in range(PASSES):
                bank = t_psum.tile([P, 512], F32, name="bank", tag="bank")
                for u in range(2):
                    for head in range(UNIT_HEADS):
                        slot = UNIT_HEADS * u + head
                        nc.tensor.transpose(
                            bank[:, P * slot : P * (slot + 1)], words[:, head, g, u, :], ident_f32[:]
                        )
                nc.scalar.copy(
                    out=grouped_words[:, 512 * g : 512 * (g + 1)].rearrange("q (f u) -> q f u", u=2),
                    in_=bank[:].rearrange("q (u f) -> q f u", u=2),
                )
            grouped_of[n] = grouped

        def quantise_unit(n):
            codes = code_pool.tile([P, PASSES * UNIT_F], U32, name="codes", align_bytes=256)
            scales = code_pool.tile([P, PASSES * UNIT_F], U8, name="scales", align_bytes=256)
            grouped = grouped_of.pop(n)
            nc.vector.quantize_mx(out=codes[:].bitcast(FP8X4), scales=scales[:], in_=grouped[:])
            codes_of[n] = (codes, scales)

        def multiply_unit(n):
            which = units[n][0]
            codes, scales = codes_of.pop(n)
            acc = acc_psum.tile([P, TOKEN_TILES * UNIT_F], F32, name="acc")
            for tt in range(TOKEN_TILES):
                for g in range(PASSES):
                    first = P * (PASSES * tt + g)
                    tokens = slice(first, first + P)
                    feats = slice(UNIT_F * g, UNIT_F * (g + 1))
                    nc.tensor.matmul_mx(
                        out=acc[:, UNIT_F * tt : UNIT_F * (tt + 1)],
                        lhsT=h_codes[:, tokens].bitcast(FP8X4),
                        lhsT_scale=h_scales[:, tokens],
                        rhs=codes[:, feats].bitcast(FP8X4),
                        rhs_scale=scales[:, feats],
                        start=(g == 0),
                        stop=(g == PASSES - 1),
                    )
            res = res_pool.tile([P, TOKEN_TILES * UNIT_F], F32, name="res")
            if which == 2:
                nc.scalar.copy(
                    out=res[:].rearrange("p (h t f) -> p t h f", h=UNIT_HEADS, t=TOKEN_TILES),
                    in_=acc[:].rearrange("p (t h f) -> p t h f", t=TOKEN_TILES, h=UNIT_HEADS),
                )
                result_of[n] = (res, None)
            else:
                both = [P, 2, TOKEN_TILES * UNIT_F]
                terms = terms_pool.tile(both, F32, name="terms")
                nc.vector.tensor_tensor(
                    out=terms[:], in0=acc[:].unsqueeze(1).to_broadcast(both),
                    in1=tables[:].rearrange("p (w c) -> p w c", w=2), op=MULT,
                )
                result_of[n] = (res, terms)

        def multiply_last_unit(n):
            which, pair = units[n]
            codes, scales = codes_of.pop(n)
            accs = [
                acc_psum.tile([P, UNIT_F], F32, name="acc_0", tag="acc"),
                t_psum.tile([P, UNIT_F], F32, name="acc_1", tag="bank"),
            ]
            for g in range(PASSES):
                for tt in range(TOKEN_TILES):
                    first = P * (PASSES * tt + g)
                    tokens = slice(first, first + P)
                    feats = slice(UNIT_F * g, UNIT_F * (g + 1))
                    nc.tensor.matmul_mx(
                        out=accs[tt][:],
                        lhsT=h_codes[:, tokens].bitcast(FP8X4),
                        lhsT_scale=h_scales[:, tokens],
                        rhs=codes[:, feats].bitcast(FP8X4),
                        rhs_scale=scales[:, feats],
                        start=(g == 0),
                        stop=(g == PASSES - 1),
                    )
            heads = outs[which][UNIT_HEADS * pair : UNIT_HEADS * (pair + 1), :, :]
            rows = heads.rearrange("h (p t) f -> p t h f", t=TOKEN_TILES)
            for tt in range(TOKEN_TILES):
                res = res_pool.tile([P, UNIT_F], F32, name="res_last%d" % tt, tag="res")
                copy = nc.scalar.copy if tt == 0 else nc.vector.tensor_copy
                copy(out=res[:], in_=accs[tt][:])
                nc.sync.dma_start(out=rows[:, tt, :, :], in_=res[:].rearrange("p (h f) -> p h f", h=UNIT_HEADS))

        def finish_unit(n):
            which, pair = units[n]
            res, terms = result_of.pop(n)
            if terms is not None:
                near = terms[:, 0, :].rearrange("p (t h s j) -> p t h s j", t=TOKEN_TILES, h=UNIT_HEADS, s=2)
                far = terms[:, 1, :].rearrange("p (t h s j) -> p t h s j", t=TOKEN_TILES, h=UNIT_HEADS, s=2)
                nc.vector.tensor_tensor(
                    out=res[:].rearrange("p (h t s j) -> p t h s j", t=TOKEN_TILES, h=UNIT_HEADS, s=2),
                    in0=near, in1=far[:, :, :, ::-1, :], op=ADD,
                )
            heads = outs[which][UNIT_HEADS * pair : UNIT_HEADS * (pair + 1), :, :]
            nc.sync.dma_start(
                out=heads.rearrange("h (p t) f -> p h (t f)", t=TOKEN_TILES),
                in_=res[:].rearrange("p (h c) -> p h c", h=UNIT_HEADS),
            )

        for n in range(PREFETCH):
            load_unit(n)
        make_tables()
        for tt in range(TOKEN_TILES):
            make_h(tt)
        for n in range(AHEAD):
            transpose_unit(n)
            if n < TOKEN_TILES:
                transpose_h(n)
                quantise_unit(n)
                quantise_h(n)
            load_unit(n + PREFETCH)
        for i in range(UNITS - 1):
            if i + 2 < UNITS:
                quantise_unit(i + 2)
            multiply_unit(i)
            if i > 0:
                finish_unit(i - 1)
            if i + AHEAD + 2 < UNITS:
                split_unit(i + AHEAD + 2)
            if i + AHEAD < UNITS:
                transpose_unit(i + AHEAD)
            if i + AHEAD + PREFETCH < UNITS:
                load_unit(i + AHEAD + PREFETCH)
        finish_unit(UNITS - 2)
        multiply_last_unit(UNITS - 1)
